import numpy as np
import ml_dtypes

BF16 = ml_dtypes.bfloat16


def bf(x):
    return np.asarray(x, np.float32).astype(BF16)


def f32(x):
    return np.asarray(x, np.float32)


def f64(x):
    return np.asarray(x).astype(np.float64)


def striped(idx):
    return np.tile(idx.reshape(-1, 16).T, (8, 1))


C, S, N, E, F, K, Q = 1024, 1024, 2048, 128, 8, 2, 4
FREQ = np.array([0.25, 0.25, 0.0625, 0.0625], np.float64)
SHIFT = np.array([0.0, np.pi / 2.0, 0.0, np.pi / 2.0], np.float64)
COORD_MAX = 6.0


def setup_inputs():
    return {"weight": f32(np.random.uniform(-1.0, 1.0, (C, S))), "coordinates": f32(np.random.uniform(-COORD_MAX, COORD_MAX, (K, N))), "offs": striped(np.random.permutation(np.tile(np.arange(S), 2))[:N])}


def reference(weight, coordinates, offs):
    idx = offs[:16].T.reshape(-1)
    emb = np.sin(f64(coordinates)[:, None, :] * FREQ[None, :, None] + SHIFT[None, :, None]).reshape(F, N)
    prod = f64(weight)[:, idx].reshape(F, E, N) * emb[:, None, :]
    return np.maximum(prod.sum(axis=0), 0.0)

@@ -1,0 +1,68 @@
+import math
+
+import concourse.mybir as mybir
+
+P = 128
+GENES = 1024
+N = 2048
+COORDS = 2
+WAVES = 4
+FEATURES = COORDS * WAVES
+PIECE = 1024
+FREQ = (0.25, 0.25, 0.0625, 0.0625)
+SHIFT = (0.0, math.pi / 2.0, 0.0, math.pi / 2.0)
+
+FLOPS = 2 * FEATURES * P * N
+
+F32 = mybir.dt.float32
+U16 = mybir.dt.uint16
+MULT = mybir.AluOpType.mult
+ADD = mybir.AluOpType.add
+SIN = mybir.ActivationFunctionType.Sin
+RELU = mybir.ActivationFunctionType.Relu
+
+
+def tile_fragmentembedder_kernel(tc, weight, coordinates, offs, out):
+    nc = tc.nc
+    with (
+        tc.tile_pool(name="held", bufs=1) as held,
+        tc.tile_pool(name="work", bufs=3) as work,
+    ):
+        offsets = held.tile([P, N // 16], U16, name="offsets")
+        nc.sync.dma_start(offsets[:], offs)
+
+        flat = coordinates.rearrange("k n -> (k n)")
+        spread = held.tile([P, COORDS * N], F32, name="spread")
+        for k in range(COORDS):
+            nc.scalar.dma_start(
+                spread[:, k * N : (k + 1) * N], flat[k * N : (k + 1) * N].partition_broadcast(P)
+            )
+
+        tables = [held.tile([P, GENES], F32, name=f"table{f}") for f in range(FEATURES)]
+        for f in range(FEATURES):
+            nc.sync.dma_start(tables[f][:], weight[f * P : (f + 1) * P, :])
+
+        for piece in range(N // PIECE):
+            first = piece * PIECE
+            piece_offsets = offsets[:, first // 16 : (first + PIECE) // 16]
+            total = work.tile([P, PIECE], F32, name="total")
+            for f in range(FEATURES):
+                k, q = divmod(f, WAVES)
+                emb = work.tile([P, PIECE], F32, name="emb")
+                nc.scalar.activation(
+                    emb[:],
+                    spread[:, k * N + first : k * N + first + PIECE],
+                    SIN,
+                    bias=SHIFT[q],
+                    scale=FREQ[q],
+                )
+                picked = tables[f][:].indirect(piece_offsets)
+                if f == 0:
+                    nc.vector.tensor_tensor(total[:], picked, emb[:], MULT)
+                else:
+                    product = work.tile([P, PIECE], F32, name="product")
+                    nc.vector.tensor_tensor(product[:], picked, emb[:], MULT)
+                    nc.vector.tensor_tensor(total[:], total[:], product[:], ADD)
+            result = work.tile([P, PIECE], F32, name="result")
+            nc.scalar.activation(result[:], total[:], RELU)
+            nc.sync.dma_start(out[:, first : first + PIECE], result[:])

@@ -1,6 +1,7 @@
 import math
 
 import concourse.mybir as mybir
+from concourse.masks import make_identity
 
 P = 128
 GENES = 1024
@@ -9,6 +10,7 @@ COORDS = 2
 WAVES = 4
 FEATURES = COORDS * WAVES
 PIECE = 1024
+BANK = 512
 FREQ = (0.25, 0.25, 0.0625, 0.0625)
 SHIFT = (0.0, math.pi / 2.0, 0.0, math.pi / 2.0)
 
@@ -17,7 +19,6 @@ FLOPS = 2 * FEATURES * P * N
 F32 = mybir.dt.float32
 U16 = mybir.dt.uint16
 MULT = mybir.AluOpType.mult
-ADD = mybir.AluOpType.add
 SIN = mybir.ActivationFunctionType.Sin
 RELU = mybir.ActivationFunctionType.Relu
 
@@ -27,6 +28,7 @@ def tile_fragmentembedder_kernel(tc, weight, coordinates, offs, out):
     with (
         tc.tile_pool(name="held", bufs=1) as held,
         tc.tile_pool(name="work", bufs=3) as work,
+        tc.psum_pool(name="psum", bufs=1) as psum,
     ):
         offsets = held.tile([P, N // 16], U16, name="offsets")
         nc.sync.dma_start(offsets[:], offs)
@@ -42,10 +44,13 @@ def tile_fragmentembedder_kernel(tc, weight, coordinates, offs, out):
         for f in range(FEATURES):
             nc.sync.dma_start(tables[f][:], weight[f * P : (f + 1) * P, :])
 
+        identity = held.tile([P, P], F32, name="identity")
+        make_identity(nc, identity[:])
+        sums = [psum.tile([P, BANK], F32, name=f"sum{b}") for b in range(N // BANK)]
+
         for piece in range(N // PIECE):
             first = piece * PIECE
             piece_offsets = offsets[:, first // 16 : (first + PIECE) // 16]
-            total = work.tile([P, PIECE], F32, name="total")
             for f in range(FEATURES):
                 k, q = divmod(f, WAVES)
                 emb = work.tile([P, PIECE], F32, name="emb")
@@ -56,13 +61,18 @@ def tile_fragmentembedder_kernel(tc, weight, coordinates, offs, out):
                     bias=SHIFT[q],
                     scale=FREQ[q],
                 )
-                picked = tables[f][:].indirect(piece_offsets)
-                if f == 0:
-                    nc.vector.tensor_tensor(total[:], picked, emb[:], MULT)
-                else:
-                    product = work.tile([P, PIECE], F32, name="product")
-                    nc.vector.tensor_tensor(product[:], picked, emb[:], MULT)
-                    nc.vector.tensor_tensor(total[:], total[:], product[:], ADD)
-            result = work.tile([P, PIECE], F32, name="result")
-            nc.scalar.activation(result[:], total[:], RELU)
-            nc.sync.dma_start(out[:, first : first + PIECE], result[:])
+                product = work.tile([P, PIECE], F32, name="product")
+                nc.vector.tensor_tensor(product[:], tables[f][:].indirect(piece_offsets), emb[:], MULT)
+                for half in range(PIECE // BANK):
+                    nc.tensor.matmul(
+                        sums[(first + half * BANK) // BANK][:],
+                        identity[:],
+                        product[:, half * BANK : (half + 1) * BANK],
+                        start=(f == 0),
+                        stop=(f == FEATURES - 1),
+                    )
+            for half in range(PIECE // BANK):
+                column = first + half * BANK
+                result = work.tile([P, BANK], F32, name="result")
+                nc.scalar.activation(result[:], sums[column // BANK][:], RELU)
+                nc.sync.dma_start(out[:, column : column + BANK], result[:])

@@ -9,8 +9,8 @@ N = 2048
 COORDS = 2
 WAVES = 4
 FEATURES = COORDS * WAVES
-PIECE = 1024
 BANK = 512
+PIECE = 2 * BANK
 FREQ = (0.25, 0.25, 0.0625, 0.0625)
 SHIFT = (0.0, math.pi / 2.0, 0.0, math.pi / 2.0)
 
@@ -21,6 +21,12 @@ U16 = mybir.dt.uint16
 MULT = mybir.AluOpType.mult
 SIN = mybir.ActivationFunctionType.Sin
 RELU = mybir.ActivationFunctionType.Relu
+
+
+def piece_widths(f):
+    if f == 0:
+        return (BANK, BANK, PIECE)
+    return (PIECE, PIECE)
 
 
 def tile_fragmentembedder_kernel(tc, weight, coordinates, offs, out):
@@ -35,9 +41,9 @@ def tile_fragmentembedder_kernel(tc, weight, coordinates, offs, out):
 
         flat = coordinates.rearrange("k n -> (k n)")
         spread = held.tile([P, COORDS * N], F32, name="spread")
-        for k in range(COORDS):
+        for first in range(0, COORDS * N, BANK):
             nc.scalar.dma_start(
-                spread[:, k * N : (k + 1) * N], flat[k * N : (k + 1) * N].partition_broadcast(P)
+                spread[:, first : first + BANK], flat[first : first + BANK].partition_broadcast(P)
             )
 
         tables = [held.tile([P, GENES], F32, name=f"table{f}") for f in range(FEATURES)]
@@ -48,31 +54,36 @@ def tile_fragmentembedder_kernel(tc, weight, coordinates, offs, out):
         make_identity(nc, identity[:])
         sums = [psum.tile([P, BANK], F32, name=f"sum{b}") for b in range(N // BANK)]
 
-        for piece in range(N // PIECE):
-            first = piece * PIECE
-            piece_offsets = offsets[:, first // 16 : (first + PIECE) // 16]
-            for f in range(FEATURES):
-                k, q = divmod(f, WAVES)
+        for f in range(FEATURES):
+            k, q = divmod(f, WAVES)
+            first = 0
+            for width in piece_widths(f):
                 emb = work.tile([P, PIECE], F32, name="emb")
                 nc.scalar.activation(
-                    emb[:],
-                    spread[:, k * N + first : k * N + first + PIECE],
+                    emb[:, :width],
+                    spread[:, k * N + first : k * N + first + width],
                     SIN,
                     bias=SHIFT[q],
                     scale=FREQ[q],
                 )
                 product = work.tile([P, PIECE], F32, name="product")
-                nc.vector.tensor_tensor(product[:], tables[f][:].indirect(piece_offsets), emb[:], MULT)
-                for half in range(PIECE // BANK):
+                nc.vector.tensor_tensor(
+                    product[:, :width],
+                    tables[f][:].indirect(offsets[:, first // 16 : (first + width) // 16]),
+                    emb[:, :width],
+                    MULT,
+                )
+                for column in range(0, width, BANK):
                     nc.tensor.matmul(
-                        sums[(first + half * BANK) // BANK][:],
+                        sums[(first + column) // BANK][:],
                         identity[:],
-                        product[:, half * BANK : (half + 1) * BANK],
+                        product[:, column : column + BANK],
                         start=(f == 0),
                         stop=(f == FEATURES - 1),
                     )
-            for half in range(PIECE // BANK):
-                column = first + half * BANK
-                result = work.tile([P, BANK], F32, name="result")
-                nc.scalar.activation(result[:], sums[column // BANK][:], RELU)
-                nc.sync.dma_start(out[:, column : column + BANK], result[:])
+                first += width
+
+        for b in range(N // BANK):
+            result = work.tile([P, BANK], F32, name="result")
+            nc.scalar.activation(result[:], sums[b][:], RELU)
+            nc.sync.dma_start(out[:, b * BANK : (b + 1) * BANK], result[:])

@@ -41,14 +41,20 @@ def tile_fragmentembedder_kernel(tc, weight, coordinates, offs, out):
 
         flat = coordinates.rearrange("k n -> (k n)")
         spread = held.tile([P, COORDS * N], F32, name="spread")
-        for first in range(0, COORDS * N, BANK):
-            nc.scalar.dma_start(
-                spread[:, first : first + BANK], flat[first : first + BANK].partition_broadcast(P)
-            )
+
+        def load_coordinates(queue, first, last):
+            queue.dma_start(spread[:, first:last], flat[first:last].partition_broadcast(P))
 
         tables = [held.tile([P, GENES], F32, name=f"table{f}") for f in range(FEATURES)]
+
+        load_coordinates(nc.scalar, 0, BANK)
         for f in range(FEATURES):
             nc.sync.dma_start(tables[f][:], weight[f * P : (f + 1) * P, :])
+            if f == 0:
+                load_coordinates(nc.sync, BANK, 2 * BANK)
+                load_coordinates(nc.sync, 2 * BANK, N)
+            if f == WAVES - 1:
+                load_coordinates(nc.sync, N, 2 * N)
 
         identity = held.tile([P, P], F32, name="identity")
         make_identity(nc, identity[:])

@@ -89,7 +89,8 @@ def tile_fragmentembedder_kernel(tc, weight, coordinates, offs, out):
                     )
                 first += width
 
+        result = held.tile([P, N], F32, name="result")
         for b in range(N // BANK):
-            result = work.tile([P, BANK], F32, name="result")
-            nc.scalar.activation(result[:], sums[b][:], RELU)
-            nc.sync.dma_start(out[:, b * BANK : (b + 1) * BANK], result[:])
+            columns = slice(b * BANK, (b + 1) * BANK)
+            nc.scalar.activation(result[:, columns], sums[b][:], RELU)
+            nc.sync.dma_start(out[:, columns], result[:, columns])

@@ -23,12 +23,6 @@ SIN = mybir.ActivationFunctionType.Sin
 RELU = mybir.ActivationFunctionType.Relu
 
 
-def piece_widths(f):
-    if f == 0:
-        return (BANK, BANK, PIECE)
-    return (PIECE, PIECE)
-
-
 def tile_fragmentembedder_kernel(tc, weight, coordinates, offs, out):
     nc = tc.nc
     with (
@@ -37,60 +31,63 @@ def tile_fragmentembedder_kernel(tc, weight, coordinates, offs, out):
         tc.psum_pool(name="psum", bufs=1) as psum,
     ):
         offsets = held.tile([P, N // 16], U16, name="offsets")
-        nc.sync.dma_start(offsets[:], offs)
-
         flat = coordinates.rearrange("k n -> (k n)")
         spread = held.tile([P, COORDS * N], F32, name="spread")
+        tables = [held.tile([P, GENES], F32, name=f"table{f}") for f in range(FEATURES)]
 
         def load_coordinates(queue, first, last):
             queue.dma_start(spread[:, first:last], flat[first:last].partition_broadcast(P))
 
-        tables = [held.tile([P, GENES], F32, name=f"table{f}") for f in range(FEATURES)]
-
         load_coordinates(nc.scalar, 0, BANK)
+        nc.sync.dma_start(offsets[:], offs)
         for f in range(FEATURES):
             nc.sync.dma_start(tables[f][:], weight[f * P : (f + 1) * P, :])
             if f == 0:
-                load_coordinates(nc.sync, BANK, 2 * BANK)
-                load_coordinates(nc.sync, 2 * BANK, N)
+                load_coordinates(nc.sync, BANK, PIECE)
             if f == WAVES - 1:
-                load_coordinates(nc.sync, N, 2 * N)
+                load_coordinates(nc.sync, N, N + PIECE)
+        for k in range(COORDS):
+            load_coordinates(nc.sync, k * N + PIECE, (k + 1) * N)
 
         identity = held.tile([P, P], F32, name="identity")
         make_identity(nc, identity[:])
         sums = [psum.tile([P, BANK], F32, name=f"sum{b}") for b in range(N // BANK)]
 
-        for f in range(FEATURES):
+        def multiply_and_add(f, first, width):
             k, q = divmod(f, WAVES)
-            first = 0
-            for width in piece_widths(f):
-                emb = work.tile([P, PIECE], F32, name="emb")
-                nc.scalar.activation(
-                    emb[:, :width],
-                    spread[:, k * N + first : k * N + first + width],
-                    SIN,
-                    bias=SHIFT[q],
-                    scale=FREQ[q],
+            emb = work.tile([P, PIECE], F32, name="emb")
+            nc.scalar.activation(
+                emb[:, :width],
+                spread[:, k * N + first : k * N + first + width],
+                SIN,
+                bias=SHIFT[q],
+                scale=FREQ[q],
+            )
+            product = work.tile([P, PIECE], F32, name="product")
+            nc.vector.tensor_tensor(
+                product[:, :width],
+                tables[f][:].indirect(offsets[:, first // 16 : (first + width) // 16]),
+                emb[:, :width],
+                MULT,
+            )
+            for column in range(0, width, BANK):
+                nc.tensor.matmul(
+                    sums[(first + column) // BANK][:],
+                    identity[:],
+                    product[:, column : column + BANK],
+                    start=(f == 0),
+                    stop=(f == FEATURES - 1),
                 )
-                product = work.tile([P, PIECE], F32, name="product")
-                nc.vector.tensor_tensor(
-                    product[:, :width],
-                    tables[f][:].indirect(offsets[:, first // 16 : (first + width) // 16]),
-                    emb[:, :width],
-                    MULT,
-                )
-                for column in range(0, width, BANK):
-                    nc.tensor.matmul(
-                        sums[(first + column) // BANK][:],
-                        identity[:],
-                        product[:, column : column + BANK],
-                        start=(f == 0),
-                        stop=(f == FEATURES - 1),
-                    )
-                first += width
 
         result = held.tile([P, N], F32, name="result")
-        for b in range(N // BANK):
-            columns = slice(b * BANK, (b + 1) * BANK)
-            nc.scalar.activation(result[:, columns], sums[b][:], RELU)
-            nc.sync.dma_start(out[:, columns], result[:, columns])
+        for first in range(0, N, PIECE):
+            for f in range(FEATURES):
+                if first == 0 and f == 0:
+                    multiply_and_add(f, 0, BANK)
+                    multiply_and_add(f, BANK, BANK)
+                else:
+                    multiply_and_add(f, first, PIECE)
+            for column in range(first, first + PIECE, BANK):
+                columns = slice(column, column + BANK)
+                nc.scalar.activation(result[:, columns], sums[column // BANK][:], RELU)
+                nc.sync.dma_start(out[:, columns], result[:, columns])

@@ -11,6 +11,7 @@ WAVES = 4
 FEATURES = COORDS * WAVES
 BANK = 512
 PIECE = 2 * BANK
+WARM_UP = 10
 FREQ = (0.25, 0.25, 0.0625, 0.0625)
 SHIFT = (0.0, math.pi / 2.0, 0.0, math.pi / 2.0)
 
@@ -52,6 +53,10 @@ def tile_fragmentembedder_kernel(tc, weight, coordinates, offs, out):
         identity = held.tile([P, P], F32, name="identity")
         make_identity(nc, identity[:])
         sums = [psum.tile([P, BANK], F32, name=f"sum{b}") for b in range(N // BANK)]
+
+        unread = psum.tile([P, P], F32, name="unread")
+        for repeat in range(WARM_UP):
+            nc.tensor.matmul(unread[:], identity[:], identity[:], start=True, stop=True)
 
         def multiply_and_add(f, first, width):
             k, q = divmod(f, WAVES)

@@ -11,7 +11,6 @@ WAVES = 4
 FEATURES = COORDS * WAVES
 BANK = 512
 PIECE = 2 * BANK
-WARM_UP = 10
 FREQ = (0.25, 0.25, 0.0625, 0.0625)
 SHIFT = (0.0, math.pi / 2.0, 0.0, math.pi / 2.0)
 
@@ -39,12 +38,10 @@ def tile_fragmentembedder_kernel(tc, weight, coordinates, offs, out):
         def load_coordinates(queue, first, last):
             queue.dma_start(spread[:, first:last], flat[first:last].partition_broadcast(P))
 
-        load_coordinates(nc.scalar, 0, BANK)
+        load_coordinates(nc.scalar, 0, PIECE)
         nc.sync.dma_start(offsets[:], offs)
         for f in range(FEATURES):
             nc.sync.dma_start(tables[f][:], weight[f * P : (f + 1) * P, :])
-            if f == 0:
-                load_coordinates(nc.sync, BANK, PIECE)
             if f == WAVES - 1:
                 load_coordinates(nc.sync, N, N + PIECE)
         for k in range(COORDS):
@@ -53,10 +50,6 @@ def tile_fragmentembedder_kernel(tc, weight, coordinates, offs, out):
         identity = held.tile([P, P], F32, name="identity")
         make_identity(nc, identity[:])
         sums = [psum.tile([P, BANK], F32, name=f"sum{b}") for b in range(N // BANK)]
-
-        unread = psum.tile([P, P], F32, name="unread")
-        for repeat in range(WARM_UP):
-            nc.tensor.matmul(unread[:], identity[:], identity[:], start=True, stop=True)
 
         def multiply_and_add(f, first, width):
             k, q = divmod(f, WAVES)
@@ -87,11 +80,7 @@ def tile_fragmentembedder_kernel(tc, weight, coordinates, offs, out):
         result = held.tile([P, N], F32, name="result")
         for first in range(0, N, PIECE):
             for f in range(FEATURES):
-                if first == 0 and f == 0:
-                    multiply_and_add(f, 0, BANK)
-                    multiply_and_add(f, BANK, BANK)
-                else:
-                    multiply_and_add(f, first, PIECE)
+                multiply_and_add(f, first, PIECE)
             for column in range(first, first + PIECE, BANK):
                 columns = slice(column, column + BANK)
                 nc.scalar.activation(result[:, columns], sums[column // BANK][:], RELU)

@@ -19,6 +19,7 @@ FLOPS = 2 * FEATURES * P * N
 F32 = mybir.dt.float32
 U16 = mybir.dt.uint16
 MULT = mybir.AluOpType.mult
+ADD = mybir.AluOpType.add
 SIN = mybir.ActivationFunctionType.Sin
 RELU = mybir.ActivationFunctionType.Relu
 
@@ -51,37 +52,50 @@ def tile_fragmentembedder_kernel(tc, weight, coordinates, offs, out):
         make_identity(nc, identity[:])
         sums = [psum.tile([P, BANK], F32, name=f"sum{b}") for b in range(N // BANK)]
 
-        def multiply_and_add(f, first, width):
+        def multiply(f, first):
             k, q = divmod(f, WAVES)
             emb = work.tile([P, PIECE], F32, name="emb")
             nc.scalar.activation(
-                emb[:, :width],
-                spread[:, k * N + first : k * N + first + width],
+                emb[:],
+                spread[:, k * N + first : k * N + first + PIECE],
                 SIN,
                 bias=SHIFT[q],
                 scale=FREQ[q],
             )
             product = work.tile([P, PIECE], F32, name="product")
             nc.vector.tensor_tensor(
-                product[:, :width],
-                tables[f][:].indirect(offsets[:, first // 16 : (first + width) // 16]),
-                emb[:, :width],
+                product[:],
+                tables[f][:].indirect(offsets[:, first // 16 : (first + PIECE) // 16]),
+                emb[:],
                 MULT,
             )
-            for column in range(0, width, BANK):
-                nc.tensor.matmul(
-                    sums[(first + column) // BANK][:],
-                    identity[:],
-                    product[:, column : column + BANK],
-                    start=(f == 0),
-                    stop=(f == FEATURES - 1),
-                )
+            return product
 
         result = held.tile([P, N], F32, name="result")
         for first in range(0, N, PIECE):
+            final_piece = first + PIECE == N
+            on_tensor = FEATURES - 1 if final_piece else FEATURES
             for f in range(FEATURES):
-                multiply_and_add(f, first, PIECE)
-            for column in range(first, first + PIECE, BANK):
-                columns = slice(column, column + BANK)
-                nc.scalar.activation(result[:, columns], sums[column // BANK][:], RELU)
+                product = multiply(f, first)
+                if f < on_tensor:
+                    for column in range(0, PIECE, BANK):
+                        nc.tensor.matmul(
+                            sums[(first + column) // BANK][:],
+                            identity[:],
+                            product[:, column : column + BANK],
+                            start=(f == 0),
+                            stop=(f == on_tensor - 1),
+                        )
+            for column in range(0, PIECE, BANK):
+                columns = slice(first + column, first + column + BANK)
+                total = sums[(first + column) // BANK]
+                if final_piece:
+                    total = work.tile([P, BANK], F32, name="total")
+                    nc.vector.tensor_tensor(
+                        total[:],
+                        sums[(first + column) // BANK][:],
+                        product[:, column : column + BANK],
+                        ADD,
+                    )
+                nc.scalar.activation(result[:, columns], total[:], RELU)
                 nc.sync.dma_start(out[:, columns], result[:, columns])

@@ -39,10 +39,12 @@ def tile_fragmentembedder_kernel(tc, weight, coordinates, offs, out):
         def load_coordinates(queue, first, last):
             queue.dma_start(spread[:, first:last], flat[first:last].partition_broadcast(P))
 
-        load_coordinates(nc.scalar, 0, PIECE)
+        load_coordinates(nc.scalar, 0, BANK)
         nc.sync.dma_start(offsets[:], offs)
         for f in range(FEATURES):
             nc.sync.dma_start(tables[f][:], weight[f * P : (f + 1) * P, :])
+            if f == 0:
+                load_coordinates(nc.sync, BANK, PIECE)
             if f == WAVES - 1:
                 load_coordinates(nc.sync, N, N + PIECE)
         for k in range(COORDS):
@@ -55,20 +57,25 @@ def tile_fragmentembedder_kernel(tc, weight, coordinates, offs, out):
         def multiply(f, first):
             k, q = divmod(f, WAVES)
             emb = work.tile([P, PIECE], F32, name="emb")
-            nc.scalar.activation(
-                emb[:],
-                spread[:, k * N + first : k * N + first + PIECE],
-                SIN,
-                bias=SHIFT[q],
-                scale=FREQ[q],
-            )
             product = work.tile([P, PIECE], F32, name="product")
-            nc.vector.tensor_tensor(
-                product[:],
-                tables[f][:].indirect(offsets[:, first // 16 : (first + PIECE) // 16]),
-                emb[:],
-                MULT,
-            )
+            width = BANK if (f == 0 and first == 0) else PIECE
+            for column in range(0, PIECE, width):
+                here = slice(column, column + width)
+                nc.scalar.activation(
+                    emb[:, here],
+                    spread[:, k * N + first + column : k * N + first + column + width],
+                    SIN,
+                    bias=SHIFT[q],
+                    scale=FREQ[q],
+                )
+                nc.vector.tensor_tensor(
+                    product[:, here],
+                    tables[f][:].indirect(
+                        offsets[:, (first + column) // 16 : (first + column + width) // 16]
+                    ),
+                    emb[:, here],
+                    MULT,
+                )
             return product
 
         result = held.tile([P, N], F32, name="result")

@@ -39,12 +39,10 @@ def tile_fragmentembedder_kernel(tc, weight, coordinates, offs, out):
         def load_coordinates(queue, first, last):
             queue.dma_start(spread[:, first:last], flat[first:last].partition_broadcast(P))
 
-        load_coordinates(nc.scalar, 0, BANK)
+        load_coordinates(nc.scalar, 0, PIECE)
         nc.sync.dma_start(offsets[:], offs)
         for f in range(FEATURES):
             nc.sync.dma_start(tables[f][:], weight[f * P : (f + 1) * P, :])
-            if f == 0:
-                load_coordinates(nc.sync, BANK, PIECE)
             if f == WAVES - 1:
                 load_coordinates(nc.sync, N, N + PIECE)
         for k in range(COORDS):

@@ -28,7 +28,7 @@ def tile_fragmentembedder_kernel(tc, weight, coordinates, offs, out):
     nc = tc.nc
     with (
         tc.tile_pool(name="held", bufs=1) as held,
-        tc.tile_pool(name="work", bufs=3) as work,
+        tc.tile_pool(name="work", bufs=5) as work,
         tc.psum_pool(name="psum", bufs=1) as psum,
     ):
         offsets = held.tile([P, N // 16], U16, name="offsets")

@@ -11,6 +11,7 @@ WAVES = 4
 FEATURES = COORDS * WAVES
 BANK = 512
 PIECE = 2 * BANK
+LAST_STEP = BANK // 2
 FREQ = (0.25, 0.25, 0.0625, 0.0625)
 SHIFT = (0.0, math.pi / 2.0, 0.0, math.pi / 2.0)
 
@@ -91,16 +92,15 @@ def tile_fragmentembedder_kernel(tc, weight, coordinates, offs, out):
                             start=(f == 0),
                             stop=(f == on_tensor - 1),
                         )
-            for column in range(0, PIECE, BANK):
-                columns = slice(first + column, first + column + BANK)
-                total = sums[(first + column) // BANK]
+            step = LAST_STEP if final_piece else BANK
+            for column in range(first, first + PIECE, step):
+                columns = slice(column, column + step)
+                total = sums[column // BANK][:, column % BANK : column % BANK + step]
                 if final_piece:
-                    total = work.tile([P, BANK], F32, name="total")
+                    added = work.tile([P, LAST_STEP], F32, name="added")
                     nc.vector.tensor_tensor(
-                        total[:],
-                        sums[(first + column) // BANK][:],
-                        product[:, column : column + BANK],
-                        ADD,
+                        added[:], total, product[:, column - first : column - first + step], ADD
                     )
-                nc.scalar.activation(result[:, columns], total[:], RELU)
+                    total = added[:]
+                nc.scalar.activation(result[:, columns], total, RELU)
                 nc.sync.dma_start(out[:, columns], result[:, columns])

@@ -41,9 +41,10 @@ def tile_fragmentembedder_kernel(tc, weight, coordinates, offs, out):
             queue.dma_start(spread[:, first:last], flat[first:last].partition_broadcast(P))
 
         load_coordinates(nc.scalar, 0, PIECE)
-        nc.sync.dma_start(offsets[:], offs)
         for f in range(FEATURES):
             nc.sync.dma_start(tables[f][:], weight[f * P : (f + 1) * P, :])
+            if f == 0:
+                nc.sync.dma_start(offsets[:], offs)
             if f == WAVES - 1:
                 load_coordinates(nc.sync, N, N + PIECE)
         for k in range(COORDS):

@@ -1,26 +1,28 @@
 import math
 
 import concourse.mybir as mybir
-from concourse.masks import make_identity
 
 P = 128
 GENES = 1024
 N = 2048
 COORDS = 2
-WAVES = 4
-FEATURES = COORDS * WAVES
+FEATURES = 8
+SHARE = P // FEATURES
+BLOCKS = P // SHARE
+QUAD = 2 * SHARE
 BANK = 512
+STEP = BANK // 2
 PIECE = 2 * BANK
-LAST_STEP = BANK // 2
-FREQ = (0.25, 0.25, 0.0625, 0.0625)
-SHIFT = (0.0, math.pi / 2.0, 0.0, math.pi / 2.0)
 
 FLOPS = 2 * FEATURES * P * N
 
 F32 = mybir.dt.float32
+I32 = mybir.dt.int32
 U16 = mybir.dt.uint16
 MULT = mybir.AluOpType.mult
 ADD = mybir.AluOpType.add
+AND = mybir.AluOpType.bitwise_and
+EQUAL = mybir.AluOpType.is_equal
 SIN = mybir.ActivationFunctionType.Sin
 RELU = mybir.ActivationFunctionType.Relu
 
@@ -31,77 +33,100 @@ def tile_fragmentembedder_kernel(tc, weight, coordinates, offs, out):
         tc.tile_pool(name="held", bufs=1) as held,
         tc.tile_pool(name="work", bufs=5) as work,
         tc.psum_pool(name="psum", bufs=1) as psum,
+        tc.psum_pool(name="spare", bufs=3) as spare,
     ):
+        coords = held.tile([COORDS, N], F32, name="coords")
+        nc.sync.dma_start(coords[:], coordinates)
         offsets = held.tile([P, N // 16], U16, name="offsets")
-        flat = coordinates.rearrange("k n -> (k n)")
-        spread = held.tile([P, COORDS * N], F32, name="spread")
-        tables = [held.tile([P, GENES], F32, name=f"table{f}") for f in range(FEATURES)]
+        nc.sync.dma_start(offsets[:], offs)
+        rows = weight.rearrange("(p b) s -> b p s", b=BLOCKS)
+        tables = [held.tile([P, GENES], F32, name=f"table{b}") for b in range(BLOCKS)]
+        order = list(range(0, BLOCKS, 2)) + list(range(1, BLOCKS, 2))
+        for b in order:
+            nc.sync.dma_start(tables[b][:], rows[b])
 
-        def load_coordinates(queue, first, last):
-            queue.dma_start(spread[:, first:last], flat[first:last].partition_broadcast(P))
+        which = held.tile([COORDS, P], I32, name="which")
+        half = P // COORDS
+        nc.gpsimd.iota(which[:], pattern=[[1, P]], base=P, channel_multiplier=-half)
+        nc.vector.tensor_single_scalar(which[:], which[:], 256 - half, AND)
+        spread = held.tile([COORDS, P], F32, name="spread")
+        nc.vector.tensor_single_scalar(spread[:], which[:], P, EQUAL)
+        number = held.tile([P, 1], I32, name="number")
+        nc.gpsimd.iota(number[:], pattern=[[0, 1]], base=0, channel_multiplier=1)
+        high = held.tile([P, 1], I32, name="high")
+        nc.vector.tensor_single_scalar(high[:], number[:], 2 * SHARE, AND)
+        freq = held.tile([P, 1], F32, name="freq")
+        nc.vector.tensor_scalar(freq[:], high[:], (0.0625 - 0.25) / (2 * SHARE), 0.25, MULT, ADD)
+        low = held.tile([P, 1], I32, name="low")
+        nc.vector.tensor_single_scalar(low[:], number[:], SHARE, AND)
+        shift = held.tile([P, 1], F32, name="shift")
+        nc.vector.tensor_single_scalar(shift[:], low[:], math.pi / 2.0 / SHARE, MULT)
+        residue = held.tile([P, SHARE], I32, name="residue")
+        nc.gpsimd.iota(residue[:], pattern=[[1, SHARE]], base=P, channel_multiplier=-1)
+        nc.vector.tensor_single_scalar(residue[:], residue[:], SHARE - 1, AND)
+        pick = held.tile([P, 3 * SHARE], F32, name="pick")
+        nc.vector.memset(pick[:], 0.0)
+        nc.vector.tensor_single_scalar(pick[:, SHARE : 2 * SHARE], residue[:], 0, EQUAL)
 
-        load_coordinates(nc.scalar, 0, PIECE)
-        for f in range(FEATURES):
-            nc.sync.dma_start(tables[f][:], weight[f * P : (f + 1) * P, :])
-            if f == 0:
-                nc.sync.dma_start(offsets[:], offs)
-            if f == WAVES - 1:
-                load_coordinates(nc.sync, N, N + PIECE)
-        for k in range(COORDS):
-            load_coordinates(nc.sync, k * N + PIECE, (k + 1) * N)
+        emb = held.tile([P, N], F32, name="emb")
 
-        identity = held.tile([P, P], F32, name="identity")
-        make_identity(nc, identity[:])
-        sums = [psum.tile([P, BANK], F32, name=f"sum{b}") for b in range(N // BANK)]
-
-        def multiply(f, first):
-            k, q = divmod(f, WAVES)
-            emb = work.tile([P, PIECE], F32, name="emb")
-            product = work.tile([P, PIECE], F32, name="product")
-            width = BANK if (f == 0 and first == 0) else PIECE
-            for column in range(0, PIECE, width):
+        def embed(first, last, width):
+            for column in range(first, last, width):
                 here = slice(column, column + width)
-                nc.scalar.activation(
-                    emb[:, here],
-                    spread[:, k * N + first + column : k * N + first + column + width],
-                    SIN,
-                    bias=SHIFT[q],
-                    scale=FREQ[q],
+                copies = spare.tile([P, BANK], F32, name="copies")
+                nc.tensor.matmul(
+                    copies[:, :width], spread[:], coords[:, here], start=True, stop=True
                 )
+                nc.scalar.activation(
+                    emb[:, here], copies[:, :width], SIN, bias=shift[:], scale=freq[:]
+                )
+
+        ranges = [(column, BANK) for column in range(0, N - BANK, BANK)]
+        ranges += [(column, STEP) for column in range(N - BANK, N, STEP)]
+        sums = [psum.tile([P, width], F32, name=f"sum{start}") for start, width in ranges]
+        result = held.tile([P, N], F32, name="result")
+
+        def look_up(b, first, cuts):
+            product = work.tile([P, PIECE], F32, name="product")
+            column = first
+            for width in cuts:
                 nc.vector.tensor_tensor(
-                    product[:, here],
-                    tables[f][:].indirect(
-                        offsets[:, (first + column) // 16 : (first + column + width) // 16]
-                    ),
-                    emb[:, here],
+                    product[:, column - first : column - first + width],
+                    tables[b][:].indirect(offsets[:, column // 16 : (column + width) // 16]),
+                    emb[:, column : column + width],
                     MULT,
                 )
-            return product
-
-        result = held.tile([P, N], F32, name="result")
-        for first in range(0, N, PIECE):
-            final_piece = first + PIECE == N
-            on_tensor = FEATURES - 1 if final_piece else FEATURES
-            for f in range(FEATURES):
-                product = multiply(f, first)
-                if f < on_tensor:
-                    for column in range(0, PIECE, BANK):
-                        nc.tensor.matmul(
-                            sums[(first + column) // BANK][:],
-                            identity[:],
-                            product[:, column : column + BANK],
-                            start=(f == 0),
-                            stop=(f == on_tensor - 1),
-                        )
-            step = LAST_STEP if final_piece else BANK
-            for column in range(first, first + PIECE, step):
-                columns = slice(column, column + step)
-                total = sums[column // BANK][:, column % BANK : column % BANK + step]
-                if final_piece:
-                    added = work.tile([P, LAST_STEP], F32, name="added")
-                    nc.vector.tensor_tensor(
-                        added[:], total, product[:, column - first : column - first + step], ADD
+                column += width
+            quad, odd = divmod(b, 2)
+            for total, (start, width) in zip(sums, ranges):
+                if first <= start < column:
+                    nc.tensor.matmul(
+                        total[quad * QUAD : (quad + 1) * QUAD, :],
+                        pick[:, SHARE - SHARE * odd : SHARE - SHARE * odd + QUAD],
+                        product[:, start - first : start - first + width],
+                        start=(odd == 0),
+                        stop=(odd == 1),
                     )
-                    total = added[:]
-                nc.scalar.activation(result[:, columns], total, RELU)
-                nc.sync.dma_start(out[:, columns], result[:, columns])
+
+        out_rows = out.rearrange("(r b) n -> b r n", b=BLOCKS)
+
+        def finish(first, last):
+            for total, (start, width) in zip(sums, ranges):
+                if first <= start < last:
+                    here = slice(start, start + width)
+                    nc.scalar.activation(result[:, here], total[:], RELU)
+                    nc.sync.dma_start(out_rows[:, :, here], result[:, here])
+
+        embed(0, PIECE, STEP)
+        look_up(order[0], 0, [STEP, STEP])
+        look_up(order[1], 0, [BANK])
+        look_up(order[0], BANK, [BANK])
+        look_up(order[1], BANK, [BANK])
+        for b in order[2:]:
+            look_up(b, 0, [PIECE])
+        embed(PIECE, N, BANK)
+        finish(0, PIECE)
+        for b in order[:-1]:
+            look_up(b, PIECE, [PIECE])
+        look_up(order[-1], PIECE, [STEP] * (PIECE // STEP))
+        finish(PIECE, N)

@@ -14,6 +14,8 @@ BANK = 512
 STEP = BANK // 2
 PIECE = 2 * BANK
 
+HALF_BITS = 6
+
 FLOPS = 2 * FEATURES * P * N
 
 F32 = mybir.dt.float32
@@ -22,6 +24,7 @@ U16 = mybir.dt.uint16
 MULT = mybir.AluOpType.mult
 ADD = mybir.AluOpType.add
 AND = mybir.AluOpType.bitwise_and
+SHIFT_RIGHT = mybir.AluOpType.arith_shift_right
 EQUAL = mybir.AluOpType.is_equal
 SIN = mybir.ActivationFunctionType.Sin
 RELU = mybir.ActivationFunctionType.Relu
@@ -33,24 +36,25 @@ def tile_fragmentembedder_kernel(tc, weight, coordinates, offs, out):
         tc.tile_pool(name="held", bufs=1) as held,
         tc.tile_pool(name="work", bufs=5) as work,
         tc.psum_pool(name="psum", bufs=1) as psum,
-        tc.psum_pool(name="spare", bufs=3) as spare,
     ):
-        coords = held.tile([COORDS, N], F32, name="coords")
-        nc.sync.dma_start(coords[:], coordinates)
-        offsets = held.tile([P, N // 16], U16, name="offsets")
-        nc.sync.dma_start(offsets[:], offs)
+        coords = [held.tile([COORDS, PIECE], F32, name=f"coords{n}") for n in range(N // PIECE)]
+        nc.sync.dma_start(coords[0][:], coordinates[:, :PIECE])
         rows = weight.rearrange("(p b) s -> b p s", b=BLOCKS)
         tables = [held.tile([P, GENES], F32, name=f"table{b}") for b in range(BLOCKS)]
         order = list(range(0, BLOCKS, 2)) + list(range(1, BLOCKS, 2))
-        for b in order:
+        offsets = held.tile([P, N // 16], U16, name="offsets")
+        for i, b in enumerate(order):
             nc.sync.dma_start(tables[b][:], rows[b])
+            if i == 0:
+                nc.sync.dma_start(offsets[:], offs)
+        nc.sync.dma_start(coords[1][:], coordinates[:, PIECE:])
 
         which = held.tile([COORDS, P], I32, name="which")
         half = P // COORDS
-        nc.gpsimd.iota(which[:], pattern=[[1, P]], base=P, channel_multiplier=-half)
-        nc.vector.tensor_single_scalar(which[:], which[:], 256 - half, AND)
+        nc.gpsimd.iota(which[:], pattern=[[1, P]], base=0, channel_multiplier=-half)
+        nc.vector.tensor_single_scalar(which[:], which[:], HALF_BITS, SHIFT_RIGHT)
         spread = held.tile([COORDS, P], F32, name="spread")
-        nc.vector.tensor_single_scalar(spread[:], which[:], P, EQUAL)
+        nc.vector.tensor_single_scalar(spread[:], which[:], 0, EQUAL)
         number = held.tile([P, 1], I32, name="number")
         nc.gpsimd.iota(number[:], pattern=[[0, 1]], base=0, channel_multiplier=1)
         high = held.tile([P, 1], I32, name="high")
@@ -70,23 +74,30 @@ def tile_fragmentembedder_kernel(tc, weight, coordinates, offs, out):
 
         emb = held.tile([P, N], F32, name="emb")
 
-        def embed(first, last, width):
-            for column in range(first, last, width):
-                here = slice(column, column + width)
-                copies = spare.tile([P, BANK], F32, name="copies")
+        def embed(first, cuts):
+            column = first
+            for bank, width in enumerate(cuts):
+                piece, start = divmod(column, PIECE)
+                copies = psum.tile([P, BANK], F32, name="copies", tag=f"late{bank}")
                 nc.tensor.matmul(
-                    copies[:, :width], spread[:], coords[:, here], start=True, stop=True
+                    copies[:, :width],
+                    spread[:],
+                    coords[piece][:, start : start + width],
+                    start=True,
+                    stop=True,
                 )
                 nc.scalar.activation(
-                    emb[:, here], copies[:, :width], SIN, bias=shift[:], scale=freq[:]
+                    emb[:, column : column + width],
+                    copies[:, :width],
+                    SIN,
+                    bias=shift[:],
+                    scale=freq[:],
                 )
+                column += width
 
-        ranges = [(column, BANK) for column in range(0, N - BANK, BANK)]
-        ranges += [(column, STEP) for column in range(N - BANK, N, STEP)]
-        sums = [psum.tile([P, width], F32, name=f"sum{start}") for start, width in ranges]
         result = held.tile([P, N], F32, name="result")
 
-        def look_up(b, first, cuts):
+        def look_up(b, first, cuts, sums):
             product = work.tile([P, PIECE], F32, name="product")
             column = first
             for width in cuts:
@@ -98,10 +109,10 @@ def tile_fragmentembedder_kernel(tc, weight, coordinates, offs, out):
                 )
                 column += width
             quad, odd = divmod(b, 2)
-            for total, (start, width) in zip(sums, ranges):
+            for start, width, total in sums:
                 if first <= start < column:
                     nc.tensor.matmul(
-                        total[quad * QUAD : (quad + 1) * QUAD, :],
+                        total[quad * QUAD : (quad + 1) * QUAD, :width],
                         pick[:, SHARE - SHARE * odd : SHARE - SHARE * odd + QUAD],
                         product[:, start - first : start - first + width],
                         start=(odd == 0),
@@ -110,23 +121,37 @@ def tile_fragmentembedder_kernel(tc, weight, coordinates, offs, out):
 
         out_rows = out.rearrange("(r b) n -> b r n", b=BLOCKS)
 
-        def finish(first, last):
-            for total, (start, width) in zip(sums, ranges):
-                if first <= start < last:
-                    here = slice(start, start + width)
-                    nc.scalar.activation(result[:, here], total[:], RELU)
-                    nc.sync.dma_start(out_rows[:, :, here], result[:, here])
+        def finish(sums):
+            for start, width, total in sums:
+                here = slice(start, start + width)
+                nc.scalar.activation(result[:, here], total[:, :width], RELU)
+                nc.sync.dma_start(out_rows[:, :, here], result[:, here])
 
-        embed(0, PIECE, STEP)
-        look_up(order[0], 0, [STEP, STEP])
-        look_up(order[1], 0, [BANK])
-        look_up(order[0], BANK, [BANK])
-        look_up(order[1], BANK, [BANK])
-        for b in order[2:]:
-            look_up(b, 0, [PIECE])
-        embed(PIECE, N, BANK)
-        finish(0, PIECE)
+        early = [
+            (start, BANK, psum.tile([P, BANK], F32, name=f"early{start}"))
+            for start in range(0, PIECE, BANK)
+        ]
+        start_cuts = [STEP // 2, STEP // 2, STEP]
+        embed(0, start_cuts + [STEP, STEP])
+        turns = 3
+        look_up(order[0], 0, start_cuts, early)
+        for b in order[1:turns]:
+            look_up(b, 0, [BANK], early)
+        for b in order[:turns]:
+            look_up(b, BANK, [BANK], early)
+        for b in order[turns:]:
+            look_up(b, 0, [PIECE], early)
+        embed(PIECE, [BANK, BANK])
+        finish(early)
+
+        end_cuts = [STEP, STEP, STEP, STEP // 2, STEP // 2]
+        late = []
+        column = PIECE
+        for bank, width in enumerate(end_cuts):
+            total = psum.tile([P, BANK], F32, name="total", tag=f"late{bank}")
+            late.append((column, width, total))
+            column += width
         for b in order[:-1]:
-            look_up(b, PIECE, [PIECE])
-        look_up(order[-1], PIECE, [STEP] * (PIECE // STEP))
-        finish(PIECE, N)
+            look_up(b, PIECE, [PIECE], late)
+        look_up(order[-1], PIECE, end_cuts, late)
+        finish(late)

@@ -9,7 +9,8 @@ COORDS = 2
 FEATURES = 8
 SHARE = P // FEATURES
 BLOCKS = P // SHARE
-QUAD = 2 * SHARE
+QUADS = 4
+QUAD = P // QUADS
 BANK = 512
 STEP = BANK // 2
 PIECE = 2 * BANK
@@ -41,11 +42,10 @@ def tile_fragmentembedder_kernel(tc, weight, coordinates, offs, out):
         nc.sync.dma_start(coords[0][:], coordinates[:, :PIECE])
         rows = weight.rearrange("(p b) s -> b p s", b=BLOCKS)
         tables = [held.tile([P, GENES], F32, name=f"table{b}") for b in range(BLOCKS)]
-        order = list(range(0, BLOCKS, 2)) + list(range(1, BLOCKS, 2))
         offsets = held.tile([P, N // 16], U16, name="offsets")
-        for i, b in enumerate(order):
+        for b in range(BLOCKS):
             nc.sync.dma_start(tables[b][:], rows[b])
-            if i == 0:
+            if b == 0:
                 nc.sync.dma_start(offsets[:], offs)
         nc.sync.dma_start(coords[1][:], coordinates[:, PIECE:])
 
@@ -65,12 +65,11 @@ def tile_fragmentembedder_kernel(tc, weight, coordinates, offs, out):
         nc.vector.tensor_single_scalar(low[:], number[:], SHARE, AND)
         shift = held.tile([P, 1], F32, name="shift")
         nc.vector.tensor_single_scalar(shift[:], low[:], math.pi / 2.0 / SHARE, MULT)
-        residue = held.tile([P, SHARE], I32, name="residue")
-        nc.gpsimd.iota(residue[:], pattern=[[1, SHARE]], base=P, channel_multiplier=-1)
-        nc.vector.tensor_single_scalar(residue[:], residue[:], SHARE - 1, AND)
-        pick = held.tile([P, 3 * SHARE], F32, name="pick")
-        nc.vector.memset(pick[:], 0.0)
-        nc.vector.tensor_single_scalar(pick[:, SHARE : 2 * SHARE], residue[:], 0, EQUAL)
+        distance = held.tile([P, QUAD + 1], I32, name="distance")
+        nc.gpsimd.iota(distance[:], pattern=[[1, QUAD + 1]], base=2 * P - 1, channel_multiplier=-2)
+        nc.vector.tensor_single_scalar(distance[:], distance[:], QUAD - 1, AND)
+        pick = held.tile([P, QUAD + 1], F32, name="pick")
+        nc.vector.tensor_single_scalar(pick[:], distance[:], 0, EQUAL)
 
         emb = held.tile([P, N], F32, name="emb")
 
@@ -108,24 +107,26 @@ def tile_fragmentembedder_kernel(tc, weight, coordinates, offs, out):
                     MULT,
                 )
                 column += width
-            quad, odd = divmod(b, 2)
+            odd, quad = divmod(b, QUADS)
             for start, width, total in sums:
                 if first <= start < column:
                     nc.tensor.matmul(
                         total[quad * QUAD : (quad + 1) * QUAD, :width],
-                        pick[:, SHARE - SHARE * odd : SHARE - SHARE * odd + QUAD],
+                        pick[:, 1 - odd : 1 - odd + QUAD],
                         product[:, start - first : start - first + width],
                         start=(odd == 0),
                         stop=(odd == 1),
                     )
 
-        out_rows = out.rearrange("(r b) n -> b r n", b=BLOCKS)
+        out_rows = out.rearrange("(m c) n -> c m n", c=QUADS)
 
         def finish(sums):
             for start, width, total in sums:
                 here = slice(start, start + width)
                 nc.scalar.activation(result[:, here], total[:, :width], RELU)
-                nc.sync.dma_start(out_rows[:, :, here], result[:, here])
+            here = slice(sums[0][0], start + width)
+            for c in range(QUADS):
+                nc.sync.dma_start(out_rows[c][:, here], result[QUAD * c : QUAD * (c + 1), here])
 
         early = [
             (start, BANK, psum.tile([P, BANK], F32, name=f"early{start}"))
@@ -134,12 +135,12 @@ def tile_fragmentembedder_kernel(tc, weight, coordinates, offs, out):
         start_cuts = [STEP // 2, STEP // 2, STEP]
         embed(0, start_cuts + [STEP, STEP])
         turns = 3
-        look_up(order[0], 0, start_cuts, early)
-        for b in order[1:turns]:
+        look_up(0, 0, start_cuts, early)
+        for b in range(1, turns):
             look_up(b, 0, [BANK], early)
-        for b in order[:turns]:
+        for b in range(turns):
             look_up(b, BANK, [BANK], early)
-        for b in order[turns:]:
+        for b in range(turns, BLOCKS):
             look_up(b, 0, [PIECE], early)
         embed(PIECE, [BANK, BANK])
         finish(early)
@@ -151,7 +152,8 @@ def tile_fragmentembedder_kernel(tc, weight, coordinates, offs, out):
             total = psum.tile([P, BANK], F32, name="total", tag=f"late{bank}")
             late.append((column, width, total))
             column += width
-        for b in order[:-1]:
+        for b in range(BLOCKS - 1):
             look_up(b, PIECE, [PIECE], late)
-        look_up(order[-1], PIECE, end_cuts, late)
-        finish(late)
+        look_up(BLOCKS - 1, PIECE, end_cuts, late)
+        finish(late[:3])
+        finish(late[3:])

@@ -132,20 +132,19 @@ def tile_fragmentembedder_kernel(tc, weight, coordinates, offs, out):
             (start, BANK, psum.tile([P, BANK], F32, name=f"early{start}"))
             for start in range(0, PIECE, BANK)
         ]
-        start_cuts = [STEP // 2, STEP // 2, STEP]
-        embed(0, start_cuts + [STEP, STEP])
-        turns = 3
-        look_up(0, 0, start_cuts, early)
-        for b in range(1, turns):
-            look_up(b, 0, [BANK], early)
-        for b in range(turns):
-            look_up(b, BANK, [BANK], early)
-        for b in range(turns, BLOCKS):
+        embed(0, [STEP] * (PIECE // STEP))
+        turns = 2
+        for first in range(0, PIECE, BANK):
+            for b in range(turns):
+                look_up(b, first, [BANK], early)
+        for b in range(turns, QUADS):
             look_up(b, 0, [PIECE], early)
         embed(PIECE, [BANK, BANK])
+        for b in range(QUADS, BLOCKS):
+            look_up(b, 0, [PIECE], early)
         finish(early)
 
-        end_cuts = [STEP, STEP, STEP, STEP // 2, STEP // 2]
+        end_cuts = [BANK, BANK]
         late = []
         column = PIECE
         for bank, width in enumerate(end_cuts):
@@ -155,5 +154,5 @@ def tile_fragmentembedder_kernel(tc, weight, coordinates, offs, out):
         for b in range(BLOCKS - 1):
             look_up(b, PIECE, [PIECE], late)
         look_up(BLOCKS - 1, PIECE, end_cuts, late)
-        finish(late[:3])
-        finish(late[3:])
+        finish(late[:1])
+        finish(late[1:])

@@ -37,6 +37,7 @@ def tile_fragmentembedder_kernel(tc, weight, coordinates, offs, out):
         tc.tile_pool(name="held", bufs=1) as held,
         tc.tile_pool(name="work", bufs=5) as work,
         tc.psum_pool(name="psum", bufs=1) as psum,
+        tc.psum_pool(name="copied", bufs=4) as copied,
     ):
         coords = [held.tile([COORDS, PIECE], F32, name=f"coords{n}") for n in range(N // PIECE)]
         nc.sync.dma_start(coords[0][:], coordinates[:, :PIECE])
@@ -75,9 +76,9 @@ def tile_fragmentembedder_kernel(tc, weight, coordinates, offs, out):
 
         def embed(first, cuts):
             column = first
-            for bank, width in enumerate(cuts):
+            for width in cuts:
                 piece, start = divmod(column, PIECE)
-                copies = psum.tile([P, BANK], F32, name="copies", tag=f"late{bank}")
+                copies = copied.tile([P, BANK], F32, name="copies")
                 nc.tensor.matmul(
                     copies[:, :width],
                     spread[:],
@@ -95,8 +96,9 @@ def tile_fragmentembedder_kernel(tc, weight, coordinates, offs, out):
                 column += width
 
         result = held.tile([P, N], F32, name="result")
+        sums = [psum.tile([P, BANK], F32, name=f"sum{n}") for n in range(N // BANK)]
 
-        def look_up(b, first, cuts, sums):
+        def look_up(b, first, cuts):
             product = work.tile([P, PIECE], F32, name="product")
             column = first
             for width in cuts:
@@ -108,51 +110,48 @@ def tile_fragmentembedder_kernel(tc, weight, coordinates, offs, out):
                 )
                 column += width
             odd, quad = divmod(b, QUADS)
-            for start, width, total in sums:
-                if first <= start < column:
+            last = column
+            column = first
+            for width in cuts if odd else [last - first]:
+                for start in range(column, column + width, BANK):
+                    bank, offset = divmod(start, BANK)
+                    end = min(offset + width, BANK)
                     nc.tensor.matmul(
-                        total[quad * QUAD : (quad + 1) * QUAD, :width],
+                        sums[bank][quad * QUAD : (quad + 1) * QUAD, offset:end],
                         pick[:, 1 - odd : 1 - odd + QUAD],
-                        product[:, start - first : start - first + width],
+                        product[:, start - first : start - first + end - offset],
                         start=(odd == 0),
-                        stop=(odd == 1),
+                        stop=(odd == 1 and end == BANK),
                     )
+                column += width
 
         out_rows = out.rearrange("(m c) n -> c m n", c=QUADS)
 
-        def finish(sums):
-            for start, width, total in sums:
-                here = slice(start, start + width)
-                nc.scalar.activation(result[:, here], total[:, :width], RELU)
-            here = slice(sums[0][0], start + width)
+        def finish(column):
+            here = slice(column, column + BANK)
+            nc.scalar.activation(result[:, here], sums[column // BANK][:], RELU)
             for c in range(QUADS):
                 nc.sync.dma_start(out_rows[c][:, here], result[QUAD * c : QUAD * (c + 1), here])
 
-        early = [
-            (start, BANK, psum.tile([P, BANK], F32, name=f"early{start}"))
-            for start in range(0, PIECE, BANK)
-        ]
         embed(0, [STEP] * (PIECE // STEP))
-        turns = 2
-        for first in range(0, PIECE, BANK):
-            for b in range(turns):
-                look_up(b, first, [BANK], early)
+        turns = 3
+        look_up(0, 0, [STEP, STEP])
+        for b in range(1, turns):
+            look_up(b, 0, [BANK])
+        for b in range(turns):
+            look_up(b, BANK, [BANK])
         for b in range(turns, QUADS):
-            look_up(b, 0, [PIECE], early)
+            look_up(b, 0, [PIECE])
         embed(PIECE, [BANK, BANK])
         for b in range(QUADS, BLOCKS):
-            look_up(b, 0, [PIECE], early)
-        finish(early)
-
-        end_cuts = [BANK, BANK]
-        late = []
-        column = PIECE
-        for bank, width in enumerate(end_cuts):
-            total = psum.tile([P, BANK], F32, name="total", tag=f"late{bank}")
-            late.append((column, width, total))
-            column += width
-        for b in range(BLOCKS - 1):
-            look_up(b, PIECE, [PIECE], late)
-        look_up(BLOCKS - 1, PIECE, end_cuts, late)
-        finish(late[:1])
-        finish(late[1:])
+            look_up(b, 0, [PIECE])
+        finish(0)
+        finish(BANK)
+        for b in range(BLOCKS - 2):
+            look_up(b, PIECE, [PIECE])
+        look_up(BLOCKS - 2, PIECE, [BANK])
+        look_up(BLOCKS - 1, PIECE, [BANK])
+        finish(PIECE)
+        look_up(BLOCKS - 2, PIECE + BANK, [BANK])
+        look_up(BLOCKS - 1, PIECE + BANK, [STEP, STEP])
+        finish(PIECE + BANK)

@@ -14,6 +14,7 @@ QUAD = P // QUADS
 BANK = 512
 STEP = BANK // 2
 PIECE = 2 * BANK
+LAST = N - BANK
 
 HALF_BITS = 6
 
@@ -37,7 +38,7 @@ def tile_fragmentembedder_kernel(tc, weight, coordinates, offs, out):
         tc.tile_pool(name="held", bufs=1) as held,
         tc.tile_pool(name="work", bufs=5) as work,
         tc.psum_pool(name="psum", bufs=1) as psum,
-        tc.psum_pool(name="copied", bufs=4) as copied,
+        tc.psum_pool(name="copied", bufs=2) as copied,
     ):
         coords = [held.tile([COORDS, PIECE], F32, name=f"coords{n}") for n in range(N // PIECE)]
         nc.sync.dma_start(coords[0][:], coordinates[:, :PIECE])
@@ -96,62 +97,89 @@ def tile_fragmentembedder_kernel(tc, weight, coordinates, offs, out):
                 column += width
 
         result = held.tile([P, N], F32, name="result")
-        sums = [psum.tile([P, BANK], F32, name=f"sum{n}") for n in range(N // BANK)]
+        sums = {c: psum.tile([P, BANK], F32, name=f"sum{c}") for c in range(0, N, BANK)}
+        last_sums = {c: psum.tile([P, STEP], F32, name=f"last{c}") for c in range(LAST, N, STEP)}
 
-        def look_up(b, first, cuts):
-            product = work.tile([P, PIECE], F32, name="product")
-            column = first
-            for width in cuts:
-                nc.vector.tensor_tensor(
-                    product[:, column - first : column - first + width],
-                    tables[b][:].indirect(offsets[:, column // 16 : (column + width) // 16]),
-                    emb[:, column : column + width],
-                    MULT,
+        def new_product():
+            return work.tile([P, PIECE], F32, name="product")
+
+        def look_up(product, b, column, width):
+            place = column % PIECE
+            nc.vector.tensor_tensor(
+                product[:, place : place + width],
+                tables[b][:].indirect(offsets[:, column // 16 : (column + width) // 16]),
+                emb[:, column : column + width],
+                MULT,
+            )
+
+        def sum_up(product, b, column, width):
+            second, quad = divmod(b, QUADS)
+            apart = quad == QUADS - 1 and column >= LAST
+            step = STEP if apart else BANK
+            for first in range(column, column + width, step):
+                total = last_sums[first] if apart else sums[first]
+                place = first % PIECE
+                nc.tensor.matmul(
+                    total[quad * QUAD : (quad + 1) * QUAD, :],
+                    pick[:, 1 - second : 1 - second + QUAD],
+                    product[:, place : place + step],
+                    start=(second == 0),
+                    stop=(second == 1),
                 )
-                column += width
-            odd, quad = divmod(b, QUADS)
-            last = column
-            column = first
-            for width in cuts if odd else [last - first]:
-                for start in range(column, column + width, BANK):
-                    bank, offset = divmod(start, BANK)
-                    end = min(offset + width, BANK)
-                    nc.tensor.matmul(
-                        sums[bank][quad * QUAD : (quad + 1) * QUAD, offset:end],
-                        pick[:, 1 - odd : 1 - odd + QUAD],
-                        product[:, start - first : start - first + end - offset],
-                        start=(odd == 0),
-                        stop=(odd == 1 and end == BANK),
-                    )
-                column += width
+
+        def whole_piece(b, first):
+            product = new_product()
+            look_up(product, b, first, PIECE)
+            for column in range(first, first + PIECE, BANK):
+                sum_up(product, b, column, BANK)
 
         out_rows = out.rearrange("(m c) n -> c m n", c=QUADS)
 
-        def finish(column):
-            here = slice(column, column + BANK)
-            nc.scalar.activation(result[:, here], sums[column // BANK][:], RELU)
-            for c in range(QUADS):
-                nc.sync.dma_start(out_rows[c][:, here], result[QUAD * c : QUAD * (c + 1), here])
+        def relu(total, rows, column, width):
+            nc.scalar.activation(result[rows, column : column + width], total[rows, :], RELU)
+
+        def store(column, quads):
+            columns = slice(column, column + BANK)
+            for c in quads:
+                nc.sync.dma_start(
+                    out_rows[c][:, columns], result[QUAD * c : QUAD * (c + 1), columns]
+                )
 
         embed(0, [STEP] * (PIECE // STEP))
-        turns = 3
-        look_up(0, 0, [STEP, STEP])
-        for b in range(1, turns):
-            look_up(b, 0, [BANK])
-        for b in range(turns):
-            look_up(b, BANK, [BANK])
-        for b in range(turns, QUADS):
-            look_up(b, 0, [PIECE])
+        turns = [new_product() for b in range(3)]
+        for column in range(0, BANK, STEP):
+            for b in range(2):
+                look_up(turns[b], b, column, STEP)
+        for b in range(2):
+            sum_up(turns[b], b, 0, BANK)
+        look_up(turns[2], 2, 0, BANK)
+        sum_up(turns[2], 2, 0, BANK)
+        for b in range(3):
+            look_up(turns[b], b, BANK, BANK)
+            sum_up(turns[b], b, BANK, BANK)
+        for b in range(3, QUADS):
+            whole_piece(b, 0)
         embed(PIECE, [BANK, BANK])
         for b in range(QUADS, BLOCKS):
-            look_up(b, 0, [PIECE])
-        finish(0)
-        finish(BANK)
+            whole_piece(b, 0)
+        for column in range(0, PIECE, BANK):
+            relu(sums[column], slice(0, P), column, BANK)
+            store(column, range(QUADS))
+
         for b in range(BLOCKS - 2):
-            look_up(b, PIECE, [PIECE])
-        look_up(BLOCKS - 2, PIECE, [BANK])
-        look_up(BLOCKS - 1, PIECE, [BANK])
-        finish(PIECE)
-        look_up(BLOCKS - 2, PIECE + BANK, [BANK])
-        look_up(BLOCKS - 1, PIECE + BANK, [STEP, STEP])
-        finish(PIECE + BANK)
+            whole_piece(b, PIECE)
+        last_two = {b: new_product() for b in range(BLOCKS - 2, BLOCKS)}
+        for b, product in last_two.items():
+            look_up(product, b, PIECE, BANK)
+            sum_up(product, b, PIECE, BANK)
+        relu(sums[PIECE], slice(0, P), PIECE, BANK)
+        store(PIECE, range(QUADS))
+        look_up(last_two[BLOCKS - 2], BLOCKS - 2, LAST, BANK)
+        sum_up(last_two[BLOCKS - 2], BLOCKS - 2, LAST, BANK)
+        relu(sums[LAST], slice(0, P - QUAD), LAST, BANK)
+        store(LAST, range(QUADS - 1))
+        for column, total in last_sums.items():
+            look_up(last_two[BLOCKS - 1], BLOCKS - 1, column, STEP)
+            sum_up(last_two[BLOCKS - 1], BLOCKS - 1, column, STEP)
+            relu(total, slice(P - QUAD, P), column, STEP)
+        store(LAST, [QUADS - 1])

@@ -38,7 +38,6 @@ def tile_fragmentembedder_kernel(tc, weight, coordinates, offs, out):
         tc.tile_pool(name="held", bufs=1) as held,
         tc.tile_pool(name="work", bufs=5) as work,
         tc.psum_pool(name="psum", bufs=1) as psum,
-        tc.psum_pool(name="copied", bufs=2) as copied,
     ):
         coords = [held.tile([COORDS, PIECE], F32, name=f"coords{n}") for n in range(N // PIECE)]
         nc.sync.dma_start(coords[0][:], coordinates[:, :PIECE])
@@ -77,9 +76,9 @@ def tile_fragmentembedder_kernel(tc, weight, coordinates, offs, out):
 
         def embed(first, cuts):
             column = first
-            for width in cuts:
+            for i, width in enumerate(cuts):
                 piece, start = divmod(column, PIECE)
-                copies = copied.tile([P, BANK], F32, name="copies")
+                copies = psum.tile([P, BANK], F32, name="copies", tag=f"apart{i}")
                 nc.tensor.matmul(
                     copies[:, :width],
                     spread[:],
@@ -98,7 +97,6 @@ def tile_fragmentembedder_kernel(tc, weight, coordinates, offs, out):
 
         result = held.tile([P, N], F32, name="result")
         sums = {c: psum.tile([P, BANK], F32, name=f"sum{c}") for c in range(0, N, BANK)}
-        last_sums = {c: psum.tile([P, STEP], F32, name=f"last{c}") for c in range(LAST, N, STEP)}
 
         def new_product():
             return work.tile([P, PIECE], F32, name="product")
@@ -114,15 +112,16 @@ def tile_fragmentembedder_kernel(tc, weight, coordinates, offs, out):
 
         def sum_up(product, b, column, width):
             second, quad = divmod(b, QUADS)
-            apart = quad == QUADS - 1 and column >= LAST
-            step = STEP if apart else BANK
-            for first in range(column, column + width, step):
-                total = last_sums[first] if apart else sums[first]
+            if column >= LAST and quad in apart:
+                parts = [part for part in apart[quad] if column <= part[0] < column + width]
+            else:
+                parts = [(column, BANK, sums[column])]
+            for first, size, total in parts:
                 place = first % PIECE
                 nc.tensor.matmul(
-                    total[quad * QUAD : (quad + 1) * QUAD, :],
+                    total[quad * QUAD : (quad + 1) * QUAD, :size],
                     pick[:, 1 - second : 1 - second + QUAD],
-                    product[:, place : place + step],
+                    product[:, place : place + size],
                     start=(second == 0),
                     stop=(second == 1),
                 )
@@ -135,8 +134,13 @@ def tile_fragmentembedder_kernel(tc, weight, coordinates, offs, out):
 
         out_rows = out.rearrange("(m c) n -> c m n", c=QUADS)
 
-        def relu(total, rows, column, width):
-            nc.scalar.activation(result[rows, column : column + width], total[rows, :], RELU)
+        def relu(total, quads, column, width, by_vector=False):
+            rows = slice(QUAD * quads[0], QUAD * (quads[-1] + 1))
+            here, summed = result[rows, column : column + width], total[rows, :width]
+            if by_vector:
+                nc.vector.tensor_scalar_max(here, summed, 0.0)
+            else:
+                nc.scalar.activation(here, summed, RELU)
 
         def store(column, quads):
             columns = slice(column, column + BANK)
@@ -163,23 +167,35 @@ def tile_fragmentembedder_kernel(tc, weight, coordinates, offs, out):
         for b in range(QUADS, BLOCKS):
             whole_piece(b, 0)
         for column in range(0, PIECE, BANK):
-            relu(sums[column], slice(0, P), column, BANK)
+            relu(sums[column], range(QUADS), column, BANK)
             store(column, range(QUADS))
+
+        last_cuts = {
+            QUADS - 2: [(LAST, BANK)],
+            QUADS - 1: [(LAST, STEP), (LAST + STEP, STEP // 2), (N - STEP // 2, STEP // 2)],
+        }
+        apart = {quad: [] for quad in last_cuts}
+        for quad, cuts in last_cuts.items():
+            for column, width in cuts:
+                bank = sum(len(parts) for parts in apart.values())
+                total = psum.tile([P, BANK], F32, name="total", tag=f"apart{bank}")
+                apart[quad].append((column, width, total))
 
         for b in range(BLOCKS - 2):
             whole_piece(b, PIECE)
+        relu(sums[LAST], range(QUADS - 2), LAST, BANK)
+        store(LAST, range(QUADS - 2))
         last_two = {b: new_product() for b in range(BLOCKS - 2, BLOCKS)}
         for b, product in last_two.items():
             look_up(product, b, PIECE, BANK)
             sum_up(product, b, PIECE, BANK)
-        relu(sums[PIECE], slice(0, P), PIECE, BANK)
+        relu(sums[PIECE], range(QUADS), PIECE, BANK)
         store(PIECE, range(QUADS))
-        look_up(last_two[BLOCKS - 2], BLOCKS - 2, LAST, BANK)
-        sum_up(last_two[BLOCKS - 2], BLOCKS - 2, LAST, BANK)
-        relu(sums[LAST], slice(0, P - QUAD), LAST, BANK)
-        store(LAST, range(QUADS - 1))
-        for column, total in last_sums.items():
-            look_up(last_two[BLOCKS - 1], BLOCKS - 1, column, STEP)
-            sum_up(last_two[BLOCKS - 1], BLOCKS - 1, column, STEP)
-            relu(total, slice(P - QUAD, P), column, STEP)
-        store(LAST, [QUADS - 1])
+        for b, product in last_two.items():
+            for column, width, total in apart[b % QUADS]:
+                look_up(product, b, column, width)
+                sum_up(product, b, column, width)
+        for quad, by_vector in ((QUADS - 2, True), (QUADS - 1, False)):
+            for column, width, total in apart[quad]:
+                relu(total, [quad], column, width, by_vector)
+            store(LAST, [quad])

import math

import concourse.mybir as mybir

P = 128
GENES = 1024
N = 2048
COORDS = 2
FEATURES = 8
SHARE = P // FEATURES
BLOCKS = P // SHARE
QUADS = 4
QUAD = P // QUADS
BANK = 512
STEP = BANK // 2
PIECE = 2 * BANK
LAST = N - BANK

HALF_BITS = 6

FLOPS = 2 * FEATURES * P * N

F32 = mybir.dt.float32
I32 = mybir.dt.int32
U16 = mybir.dt.uint16
MULT = mybir.AluOpType.mult
ADD = mybir.AluOpType.add
AND = mybir.AluOpType.bitwise_and
SHIFT_RIGHT = mybir.AluOpType.arith_shift_right
EQUAL = mybir.AluOpType.is_equal
SIN = mybir.ActivationFunctionType.Sin
RELU = mybir.ActivationFunctionType.Relu


def tile_fragmentembedder_kernel(tc, weight, coordinates, offs, out):
    nc = tc.nc
    with (
        tc.tile_pool(name="held", bufs=1) as held,
        tc.tile_pool(name="work", bufs=5) as work,
        tc.psum_pool(name="psum", bufs=1) as psum,
    ):
        coords = [held.tile([COORDS, PIECE], F32, name=f"coords{n}") for n in range(N // PIECE)]
        nc.sync.dma_start(coords[0][:], coordinates[:, :PIECE])
        rows = weight.rearrange("(p b) s -> b p s", b=BLOCKS)
        tables = [held.tile([P, GENES], F32, name=f"table{b}") for b in range(BLOCKS)]
        offsets = held.tile([P, N // 16], U16, name="offsets")
        for b in range(BLOCKS):
            nc.sync.dma_start(tables[b][:], rows[b])
            if b == 0:
                nc.sync.dma_start(offsets[:], offs)
        nc.sync.dma_start(coords[1][:], coordinates[:, PIECE:])

        which = held.tile([COORDS, P], I32, name="which")
        half = P // COORDS
        nc.gpsimd.iota(which[:], pattern=[[1, P]], base=0, channel_multiplier=-half)
        nc.vector.tensor_single_scalar(which[:], which[:], HALF_BITS, SHIFT_RIGHT)
        spread = held.tile([COORDS, P], F32, name="spread")
        nc.vector.tensor_single_scalar(spread[:], which[:], 0, EQUAL)
        number = held.tile([P, 1], I32, name="number")
        nc.gpsimd.iota(number[:], pattern=[[0, 1]], base=0, channel_multiplier=1)
        high = held.tile([P, 1], I32, name="high")
        nc.vector.tensor_single_scalar(high[:], number[:], 2 * SHARE, AND)
        freq = held.tile([P, 1], F32, name="freq")
        nc.vector.tensor_scalar(freq[:], high[:], (0.0625 - 0.25) / (2 * SHARE), 0.25, MULT, ADD)
        low = held.tile([P, 1], I32, name="low")
        nc.vector.tensor_single_scalar(low[:], number[:], SHARE, AND)
        shift = held.tile([P, 1], F32, name="shift")
        nc.vector.tensor_single_scalar(shift[:], low[:], math.pi / 2.0 / SHARE, MULT)
        distance = held.tile([P, QUAD + 1], I32, name="distance")
        nc.gpsimd.iota(distance[:], pattern=[[1, QUAD + 1]], base=2 * P - 1, channel_multiplier=-2)
        nc.vector.tensor_single_scalar(distance[:], distance[:], QUAD - 1, AND)
        pick = held.tile([P, QUAD + 1], F32, name="pick")
        nc.vector.tensor_single_scalar(pick[:], distance[:], 0, EQUAL)

        emb = held.tile([P, N], F32, name="emb")

        def embed(first, cuts):
            column = first
            for i, width in enumerate(cuts):
                piece, start = divmod(column, PIECE)
                copies = psum.tile([P, BANK], F32, name="copies", tag=f"apart{i}")
                nc.tensor.matmul(
                    copies[:, :width],
                    spread[:],
                    coords[piece][:, start : start + width],
                    start=True,
                    stop=True,
                )
                nc.scalar.activation(
                    emb[:, column : column + width],
                    copies[:, :width],
                    SIN,
                    bias=shift[:],
                    scale=freq[:],
                )
                column += width

        result = held.tile([P, N], F32, name="result")
        sums = {c: psum.tile([P, BANK], F32, name=f"sum{c}") for c in range(0, N, BANK)}

        def new_product():
            return work.tile([P, PIECE], F32, name="product")

        def look_up(product, b, column, width):
            place = column % PIECE
            nc.vector.tensor_tensor(
                product[:, place : place + width],
                tables[b][:].indirect(offsets[:, column // 16 : (column + width) // 16]),
                emb[:, column : column + width],
                MULT,
            )

        def sum_up(product, b, column, width):
            second, quad = divmod(b, QUADS)
            if column >= LAST and quad in apart:
                parts = [part for part in apart[quad] if column <= part[0] < column + width]
            else:
                parts = [(column, BANK, sums[column])]
            for first, size, total in parts:
                place = first % PIECE
                nc.tensor.matmul(
                    total[quad * QUAD : (quad + 1) * QUAD, :size],
                    pick[:, 1 - second : 1 - second + QUAD],
                    product[:, place : place + size],
                    start=(second == 0),
                    stop=(second == 1),
                )

        def whole_piece(b, first):
            product = new_product()
            look_up(product, b, first, PIECE)
            for column in range(first, first + PIECE, BANK):
                sum_up(product, b, column, BANK)

        out_rows = out.rearrange("(m c) n -> c m n", c=QUADS)

        def relu(total, quads, column, width, by_vector=False):
            rows = slice(QUAD * quads[0], QUAD * (quads[-1] + 1))
            here, summed = result[rows, column : column + width], total[rows, :width]
            if by_vector:
                nc.vector.tensor_scalar_max(here, summed, 0.0)
            else:
                nc.scalar.activation(here, summed, RELU)

        def store(column, quads):
            columns = slice(column, column + BANK)
            for c in quads:
                nc.sync.dma_start(
                    out_rows[c][:, columns], result[QUAD * c : QUAD * (c + 1), columns]
                )

        embed(0, [STEP] * (PIECE // STEP))
        turns = [new_product() for b in range(3)]
        for column in range(0, BANK, STEP):
            for b in range(2):
                look_up(turns[b], b, column, STEP)
        for b in range(2):
            sum_up(turns[b], b, 0, BANK)
        look_up(turns[2], 2, 0, BANK)
        sum_up(turns[2], 2, 0, BANK)
        for b in range(3):
            look_up(turns[b], b, BANK, BANK)
            sum_up(turns[b], b, BANK, BANK)
        for b in range(3, QUADS):
            whole_piece(b, 0)
        embed(PIECE, [BANK, BANK])
        for b in range(QUADS, BLOCKS):
            whole_piece(b, 0)
        for column in range(0, PIECE, BANK):
            relu(sums[column], range(QUADS), column, BANK)
            store(column, range(QUADS))

        last_cuts = {
            QUADS - 2: [(LAST, BANK)],
            QUADS - 1: [(LAST, STEP), (LAST + STEP, STEP // 2), (N - STEP // 2, STEP // 2)],
        }
        apart = {quad: [] for quad in last_cuts}
        for quad, cuts in last_cuts.items():
            for column, width in cuts:
                bank = sum(len(parts) for parts in apart.values())
                total = psum.tile([P, BANK], F32, name="total", tag=f"apart{bank}")
                apart[quad].append((column, width, total))

        for b in range(BLOCKS - 2):
            whole_piece(b, PIECE)
        relu(sums[LAST], range(QUADS - 2), LAST, BANK)
        store(LAST, range(QUADS - 2))
        last_two = {b: new_product() for b in range(BLOCKS - 2, BLOCKS)}
        for b, product in last_two.items():
            look_up(product, b, PIECE, BANK)
            sum_up(product, b, PIECE, BANK)
        relu(sums[PIECE], range(QUADS), PIECE, BANK)
        store(PIECE, range(QUADS))
        for b, product in last_two.items():
            for column, width, total in apart[b % QUADS]:
                look_up(product, b, column, width)
                sum_up(product, b, column, width)
        for quad, by_vector in ((QUADS - 2, True), (QUADS - 1, False)):
            for column, width, total in apart[quad]:
                relu(total, [quad], column, width, by_vector)
            store(LAST, [quad])
